import numpy as np
import ml_dtypes


def mxq(x, axis, fmt="e4m3"):
    dtype, down = {"e4m3": (ml_dtypes.float8_e4m3fn, 7), "e5m2": (ml_dtypes.float8_e5m2, 14)}[fmt]
    v = np.moveaxis(np.asarray(x, np.float32).astype(ml_dtypes.bfloat16).astype(np.float64), axis, -1)
    blocks = v.reshape(v.shape[:-1] + (-1, 32))
    amax = np.abs(blocks).max(-1, keepdims=True)
    byte = np.maximum(np.where(amax > 0, np.frexp(amax)[1] - 1 + 127, 0) - down, 1)
    scale = np.exp2(byte - 127.0)
    codes = (blocks / scale).astype(np.float32).astype(dtype).astype(np.float64)
    return np.moveaxis((codes * scale).reshape(v.shape), -1, axis)


WIDE = False


def mx_kscale(k):
    if not WIDE:
        return np.ones(k)
    levels = np.array([10, -10, 5, -5, 0])
    a = np.random.permutation(np.resize(levels, k // 512 * 4)).reshape(k // 512, 4)
    idx = np.arange(k)
    return np.exp2(a[idx // 512, idx % 128 // 32])


BF16 = ml_dtypes.bfloat16


def bf(x):
    return np.asarray(x, np.float32).astype(BF16)


def f64(x):
    return np.asarray(x).astype(np.float64)


B, U, I, O = 128, 4, 512, 128


def sigmoid(v):
    return 1.0 / (1.0 + np.exp(-v))


def setup_inputs():
    s = mx_kscale(I)
    wi = lambda: bf(np.random.standard_normal((U, I, O)) / np.sqrt(I) / s[None, :, None])
    wh = lambda: bf(np.random.standard_normal((U, O, O)) / np.sqrt(O))
    return {"x": bf(np.random.standard_normal((B, U, I)) * s),
            "h": bf(np.random.standard_normal((B, U, O))),
            "w_ir": wi(), "w_iz": wi(), "w_in": wi(),
            "w_hr": wh(), "w_hz": wh(), "w_hn": wh()}


def reference(x, h, w_ir, w_iz, w_in, w_hr, w_hz, w_hn):
    xq = mxq(f64(x).transpose(1, 0, 2), 2, "e4m3")
    hu = f64(h).transpose(1, 0, 2)
    r = sigmoid((xq @ mxq(f64(w_ir), 1, "e4m3")) + hu @ f64(w_hr))
    z = sigmoid((xq @ mxq(f64(w_iz), 1, "e4m3")) + hu @ f64(w_hz))
    n = np.tanh((xq @ mxq(f64(w_in), 1, "e4m3")) + r * (hu @ f64(w_hn)))
    return ((1.0 - z) * n + z * hu).transpose(1, 0, 2)

@@ -1,0 +1,167 @@
+from concourse import mybir
+from concourse.masks import make_identity
+
+F32 = mybir.dt.float32
+BF16 = mybir.dt.bfloat16
+U32 = mybir.dt.uint32
+U8 = mybir.dt.uint8
+FP8X4 = mybir.dt.float8_e4m3fn_x4
+ALU = mybir.AluOpType
+ACT = mybir.ActivationFunctionType
+
+P = 128
+UNITS = 4
+IN = 512
+OUT = 128
+PACK = 4
+HALVES = 2
+UH = UNITS // HALVES
+WORDS = IN // 2
+
+FLOPS = 2 * P * UNITS * (IN + OUT) * OUT * 3
+
+
+def tile_unitwisegru_pa_s_kernel(tc, x, h, w_ir, w_iz, w_in, w_hr, w_hz, w_hn, out):
+    nc = tc.nc
+    with (
+        tc.tile_pool(name="keep", bufs=1) as keep,
+        tc.psum_pool(name="early", bufs=3) as early,
+        tc.psum_pool(name="sums", bufs=1) as sums,
+    ):
+        x_sb = keep.tile([P, UNITS * IN], BF16)
+        nc.sync.dma_start(out=x_sb[:], in_=x.rearrange("b u i -> b (u i)"))
+
+        def load_input_weight(w, half, name):
+            raw = keep.tile([P, UH, PACK, OUT], BF16, name=name)
+            units = slice(half * UH, (half + 1) * UH)
+            nc.sync.dma_start(out=raw[:], in_=w[units].rearrange("u (p j) o -> p u j o", j=PACK))
+            return raw
+
+        raw_r = [None, None]
+        raw_z = [None, None]
+        raw_n = [None, None]
+        raw_r[0] = load_input_weight(w_ir, 0, "raw_r0")
+        raw_z[0] = load_input_weight(w_iz, 0, "raw_z0")
+
+        h_sb = keep.tile([P, UNITS * OUT], BF16)
+        nc.sync.dma_start(out=h_sb[:], in_=h.rearrange("b u o -> b (u o)"))
+        wh_sb = keep.tile([P, UNITS, 3, OUT], BF16)
+        for gate, w in enumerate((w_hr, w_hz, w_hn)):
+            nc.sync.dma_start(out=wh_sb[:, :, gate, :], in_=w.rearrange("u k o -> k u o"))
+
+        raw_n[0] = load_input_weight(w_in, 0, "raw_n0")
+        raw_r[1] = load_input_weight(w_ir, 1, "raw_r1")
+        raw_z[1] = load_input_weight(w_iz, 1, "raw_z1")
+        raw_n[1] = load_input_weight(w_in, 1, "raw_n1")
+
+        ident_f32 = keep.tile([P, P], F32)
+        make_identity(nc, ident_f32[:])
+        ident_bf16 = keep.tile([P, P], BF16)
+        make_identity(nc, ident_bf16[:])
+        warm_in = keep.tile([P, 1], F32)
+        warm_out = keep.tile([P, 1], F32)
+        nc.vector.memset(warm_in[:], 0.0)
+        nc.scalar.activation(out=warm_out[:], in_=warm_in[:], func=ACT.Sigmoid)
+
+        x_words = x_sb[:].bitcast(F32).rearrange("b (u p v) -> b u v p", u=UNITS, v=2)
+        x_grouped = keep.tile([P, UNITS * P * PACK], BF16, align_bytes=64)
+        x_grouped_words = x_grouped[:].bitcast(F32).rearrange("p (u b v) -> p u b v", u=UNITS, v=2)
+        for half in range(HALVES):
+            xT = early.tile([P, UH, 2, P], F32, tag="early")
+            for uu in range(UH):
+                for v in range(2):
+                    nc.tensor.transpose(xT[:, uu, v, :], x_words[:, half * UH + uu, v, :], ident_f32[:])
+            nc.scalar.copy(
+                out=x_grouped_words[:, half * UH : (half + 1) * UH, :, :],
+                in_=xT[:].rearrange("p u v b -> p u b v"),
+            )
+        x_codes = keep.tile([P, UNITS * P], U32, align_bytes=64)
+        x_scales = keep.tile([P, UNITS * P], U8, align_bytes=64)
+        nc.vector.quantize_mx(out=x_codes[:].bitcast(FP8X4), scales=x_scales[:], in_=x_grouped[:])
+
+        hT_ps = early.tile([P, UNITS, P], BF16, tag="early")
+        for u in range(UNITS):
+            nc.tensor.transpose(hT_ps[:, u, :], h_sb[:, u * OUT : (u + 1) * OUT], ident_bf16[:])
+        hT = keep.tile([P, UNITS, P], BF16)
+        nc.scalar.copy(out=hT[:], in_=hT_ps[:])
+
+        hn_ps = sums.tile([P, UNITS, OUT], F32)
+        hrz = []
+        for half in range(HALVES):
+            hrz_ps = early.tile([P, UH, 2 * OUT], F32, tag="early")
+            for uu in range(UH):
+                u = half * UH + uu
+                nc.tensor.matmul(hrz_ps[:, uu, :], lhsT=hT[:, u, :], rhs=wh_sb[:, u, 0:2, :], start=True, stop=True)
+                nc.tensor.matmul(hn_ps[:, u, :], lhsT=hT[:, u, :], rhs=wh_sb[:, u, 2, :], start=True, stop=True)
+            hrz_sb = keep.tile([P, UH, 2 * OUT], F32, name="hrz%d" % half)
+            nc.scalar.copy(out=hrz_sb[:], in_=hrz_ps[:])
+            hrz.append(hrz_sb)
+
+        for half in range(HALVES):
+            rz_grouped = keep.tile([P, UH, 2, OUT, PACK], BF16, name="rz_grouped%d" % half, align_bytes=64)
+            n_grouped = keep.tile([P, UH, OUT, PACK], BF16, name="n_grouped%d" % half, align_bytes=64)
+            nc.vector.tensor_copy(
+                out=rz_grouped[:, :, 0, :, :].rearrange("p u (c i) j -> p u c j i", i=4),
+                in_=raw_r[half][:].rearrange("p u j (c i) -> p u c j i", i=4),
+            )
+            for uu in range(UH):
+                nc.scalar.copy(
+                    out=rz_grouped[:, uu, 1, :, :].rearrange("p (c i) j -> p c j i", i=4),
+                    in_=raw_z[half][:, uu, :, :].rearrange("p j (c i) -> p c j i", i=4),
+                )
+            nc.vector.tensor_copy(
+                out=n_grouped[:].rearrange("p u (c i) j -> p u c j i", i=4),
+                in_=raw_n[half][:].rearrange("p u j (c i) -> p u c j i", i=4),
+            )
+
+            rz_codes = keep.tile([P, UH, 2 * OUT], U32, name="rz_codes%d" % half, align_bytes=64)
+            rz_scales = keep.tile([P, UH, 2 * OUT], U8, name="rz_scales%d" % half, align_bytes=64)
+            nc.vector.quantize_mx(
+                out=rz_codes[:].rearrange("p u c -> p (u c)").bitcast(FP8X4),
+                scales=rz_scales[:].rearrange("p u c -> p (u c)"),
+                in_=rz_grouped[:].rearrange("p u g o j -> p (u g o j)"),
+            )
+            n_codes = keep.tile([P, UH, OUT], U32, name="n_codes%d" % half, align_bytes=64)
+            n_scales = keep.tile([P, UH, OUT], U8, name="n_scales%d" % half, align_bytes=64)
+            nc.vector.quantize_mx(
+                out=n_codes[:].rearrange("p u c -> p (u c)").bitcast(FP8X4),
+                scales=n_scales[:].rearrange("p u c -> p (u c)"),
+                in_=n_grouped[:].rearrange("p u o j -> p (u o j)"),
+            )
+
+            xrz_ps = sums.tile([P, UH, 2 * OUT], F32, name="xrz_ps%d" % half)
+            xn_ps = sums.tile([P, UH, OUT], F32, name="xn_ps%d" % half)
+            for codes, scales, acc in ((rz_codes, rz_scales, xrz_ps), (n_codes, n_scales, xn_ps)):
+                for uu in range(UH):
+                    batch = slice((half * UH + uu) * P, (half * UH + uu + 1) * P)
+                    nc.tensor.matmul_mx(
+                        out=acc[:, uu, :],
+                        lhsT=x_codes[:, batch].bitcast(FP8X4),
+                        lhsT_scale=x_scales[:, batch],
+                        rhs=codes[:, uu, :].bitcast(FP8X4),
+                        rhs_scale=scales[:, uu, :],
+                        start=True,
+                        stop=True,
+                    )
+
+            units = slice(half * UH, (half + 1) * UH)
+            rz = keep.tile([P, UH, 2, OUT], F32, name="rz%d" % half)
+            rz_flat = rz[:].rearrange("p u g o -> p u (g o)")
+            nc.vector.tensor_tensor(out=rz_flat, in0=xrz_ps[:], in1=hrz[half][:], op=ALU.add)
+            nc.scalar.activation(out=rz_flat, in_=rz_flat, func=ACT.Sigmoid)
+            r = rz[:, :, 0, :]
+            z = rz[:, :, 1, :]
+
+            n = keep.tile([P, UH, OUT], F32, name="n%d" % half)
+            nc.vector.tensor_tensor(out=n[:], in0=r, in1=hn_ps[:, units, :], op=ALU.mult)
+            nc.vector.tensor_tensor(out=n[:], in0=n[:], in1=xn_ps[:], op=ALU.add)
+            nc.scalar.activation(out=n[:], in_=n[:], func=ACT.Tanh)
+
+            zh = keep.tile([P, UH, OUT], F32, name="zh%d" % half)
+            h_half = h_sb[:].rearrange("b (u o) -> b u o", u=UNITS)[:, units, :]
+            nc.vector.tensor_tensor(out=zh[:], in0=z, in1=h_half, op=ALU.mult)
+            zn = keep.tile([P, UH, OUT], F32, name="zn%d" % half)
+            nc.vector.scalar_tensor_tensor(out=zn[:], in0=z, scalar=1.0, in1=n[:], op0=ALU.subtract, op1=ALU.mult)
+            result = keep.tile([P, UH, OUT], F32, name="result%d" % half)
+            nc.vector.tensor_tensor(out=result[:], in0=zh[:], in1=zn[:], op=ALU.subtract)
+            nc.sync.dma_start(out=out[:, units, :], in_=result[:])

@@ -16,43 +16,54 @@ OUT = 128
 PACK = 4
 HALVES = 2
 UH = UNITS // HALVES
-WORDS = IN // 2
 
 FLOPS = 2 * P * UNITS * (IN + OUT) * OUT * 3
+
+
+def units_of(half):
+    return slice(half * UH, (half + 1) * UH)
 
 
 def tile_unitwisegru_pa_s_kernel(tc, x, h, w_ir, w_iz, w_in, w_hr, w_hz, w_hn, out):
     nc = tc.nc
     with (
         tc.tile_pool(name="keep", bufs=1) as keep,
-        tc.psum_pool(name="early", bufs=3) as early,
-        tc.psum_pool(name="sums", bufs=1) as sums,
+        tc.psum_pool(name="psum", bufs=8) as psum,
+        tc.manual_schedule(),
     ):
-        x_sb = keep.tile([P, UNITS * IN], BF16)
-        nc.sync.dma_start(out=x_sb[:], in_=x.rearrange("b u i -> b (u i)"))
+        def bank(shape, dtype, name):
+            return psum.tile(shape, dtype, name=name, tag="bank")
 
-        def load_input_weight(w, half, name):
-            raw = keep.tile([P, UH, PACK, OUT], BF16, name=name)
-            units = slice(half * UH, (half + 1) * UH)
-            nc.sync.dma_start(out=raw[:], in_=w[units].rearrange("u (p j) o -> p u j o", j=PACK))
-            return raw
+        def f32_halves(name):
+            return [keep.tile([P, UH, OUT], F32, name="%s%d" % (name, half)) for half in range(HALVES)]
 
-        raw_r = [None, None]
-        raw_z = [None, None]
-        raw_n = [None, None]
-        raw_r[0] = load_input_weight(w_ir, 0, "raw_r0")
-        raw_z[0] = load_input_weight(w_iz, 0, "raw_z0")
+        x_sb = keep.tile([P, UNITS, IN], BF16)
+        h_sb = keep.tile([P, UNITS, OUT], BF16)
+        raw = {}
+        wh_sb = {}
+        for gate in "rnz":
+            raw[gate] = keep.tile([P, UNITS, PACK, OUT], BF16, name="raw_" + gate)
+            wh_sb[gate] = keep.tile([P, UNITS, OUT], BF16, name="wh_" + gate)
 
-        h_sb = keep.tile([P, UNITS * OUT], BF16)
-        nc.sync.dma_start(out=h_sb[:], in_=h.rearrange("b u o -> b (u o)"))
-        wh_sb = keep.tile([P, UNITS, 3, OUT], BF16)
-        for gate, w in enumerate((w_hr, w_hz, w_hn)):
-            nc.sync.dma_start(out=wh_sb[:, :, gate, :], in_=w.rearrange("u k o -> k u o"))
+        def load_input_weight(gate, w):
+            for half in range(HALVES):
+                nc.sync.dma_start(
+                    out=raw[gate][:, units_of(half), :, :],
+                    in_=w[units_of(half)].rearrange("u (p j) o -> p u j o", j=PACK),
+                )
 
-        raw_n[0] = load_input_weight(w_in, 0, "raw_n0")
-        raw_r[1] = load_input_weight(w_ir, 1, "raw_r1")
-        raw_z[1] = load_input_weight(w_iz, 1, "raw_z1")
-        raw_n[1] = load_input_weight(w_in, 1, "raw_n1")
+        def load_hidden_weight(gate, w):
+            nc.sync.dma_start(out=wh_sb[gate][:], in_=w.rearrange("u k o -> k u o"))
+
+        for half in range(HALVES):
+            nc.sync.dma_start(out=x_sb[:, units_of(half), :], in_=x[:, units_of(half), :])
+        load_input_weight("r", w_ir)
+        nc.sync.dma_start(out=h_sb[:], in_=h)
+        load_hidden_weight("r", w_hr)
+        load_hidden_weight("n", w_hn)
+        load_input_weight("n", w_in)
+        load_hidden_weight("z", w_hz)
+        load_input_weight("z", w_iz)
 
         ident_f32 = keep.tile([P, P], F32)
         make_identity(nc, ident_f32[:])
@@ -63,105 +74,116 @@ def tile_unitwisegru_pa_s_kernel(tc, x, h, w_ir, w_iz, w_in, w_hr, w_hz, w_hn, o
         nc.vector.memset(warm_in[:], 0.0)
         nc.scalar.activation(out=warm_out[:], in_=warm_in[:], func=ACT.Sigmoid)
 
-        x_words = x_sb[:].bitcast(F32).rearrange("b (u p v) -> b u v p", u=UNITS, v=2)
-        x_grouped = keep.tile([P, UNITS * P * PACK], BF16, align_bytes=64)
-        x_grouped_words = x_grouped[:].bitcast(F32).rearrange("p (u b v) -> p u b v", u=UNITS, v=2)
-        for half in range(HALVES):
-            xT = early.tile([P, UH, 2, P], F32, tag="early")
-            for uu in range(UH):
-                for v in range(2):
-                    nc.tensor.transpose(xT[:, uu, v, :], x_words[:, half * UH + uu, v, :], ident_f32[:])
-            nc.scalar.copy(
-                out=x_grouped_words[:, half * UH : (half + 1) * UH, :, :],
-                in_=xT[:].rearrange("p u v b -> p u b v"),
-            )
-        x_codes = keep.tile([P, UNITS * P], U32, align_bytes=64)
-        x_scales = keep.tile([P, UNITS * P], U8, align_bytes=64)
-        nc.vector.quantize_mx(out=x_codes[:].bitcast(FP8X4), scales=x_scales[:], in_=x_grouped[:])
+        grouped = {}
+        codes = {}
+        scales = {}
+        for gate in "rnz":
+            grouped[gate] = keep.tile([P, UNITS, OUT, PACK], BF16, name="grouped_" + gate, align_bytes=64)
+            codes[gate] = keep.tile([P, UNITS, OUT], U32, name="codes_" + gate, align_bytes=64)
+            scales[gate] = keep.tile([P, UNITS, OUT], U8, name="scales_" + gate, align_bytes=64)
 
-        hT_ps = early.tile([P, UNITS, P], BF16, tag="early")
-        for u in range(UNITS):
-            nc.tensor.transpose(hT_ps[:, u, :], h_sb[:, u * OUT : (u + 1) * OUT], ident_bf16[:])
-        hT = keep.tile([P, UNITS, P], BF16)
-        nc.scalar.copy(out=hT[:], in_=hT_ps[:])
+        def regroup(gate):
+            for half in range(HALVES):
+                for uu, copy in enumerate((nc.vector.tensor_copy, nc.scalar.copy)):
+                    u = half * UH + uu
+                    copy(
+                        out=grouped[gate][:, u, :, :].rearrange("p (c i) j -> p c j i", i=4),
+                        in_=raw[gate][:, u, :, :].rearrange("p j (c i) -> p c j i", i=4),
+                    )
 
-        hn_ps = sums.tile([P, UNITS, OUT], F32)
-        hrz = []
-        for half in range(HALVES):
-            hrz_ps = early.tile([P, UH, 2 * OUT], F32, tag="early")
-            for uu in range(UH):
-                u = half * UH + uu
-                nc.tensor.matmul(hrz_ps[:, uu, :], lhsT=hT[:, u, :], rhs=wh_sb[:, u, 0:2, :], start=True, stop=True)
-                nc.tensor.matmul(hn_ps[:, u, :], lhsT=hT[:, u, :], rhs=wh_sb[:, u, 2, :], start=True, stop=True)
-            hrz_sb = keep.tile([P, UH, 2 * OUT], F32, name="hrz%d" % half)
-            nc.scalar.copy(out=hrz_sb[:], in_=hrz_ps[:])
-            hrz.append(hrz_sb)
-
-        for half in range(HALVES):
-            rz_grouped = keep.tile([P, UH, 2, OUT, PACK], BF16, name="rz_grouped%d" % half, align_bytes=64)
-            n_grouped = keep.tile([P, UH, OUT, PACK], BF16, name="n_grouped%d" % half, align_bytes=64)
-            nc.vector.tensor_copy(
-                out=rz_grouped[:, :, 0, :, :].rearrange("p u (c i) j -> p u c j i", i=4),
-                in_=raw_r[half][:].rearrange("p u j (c i) -> p u c j i", i=4),
-            )
-            for uu in range(UH):
-                nc.scalar.copy(
-                    out=rz_grouped[:, uu, 1, :, :].rearrange("p (c i) j -> p c j i", i=4),
-                    in_=raw_z[half][:, uu, :, :].rearrange("p j (c i) -> p c j i", i=4),
+        def x_times_weight(gate):
+            for half in range(HALVES):
+                nc.vector.quantize_mx(
+                    out=codes[gate][:, units_of(half), :].rearrange("p u o -> p (u o)").bitcast(FP8X4),
+                    scales=scales[gate][:, units_of(half), :].rearrange("p u o -> p (u o)"),
+                    in_=grouped[gate][:, units_of(half), :, :].rearrange("p u o j -> p (u o j)"),
                 )
-            nc.vector.tensor_copy(
-                out=n_grouped[:].rearrange("p u (c i) j -> p u c j i", i=4),
-                in_=raw_n[half][:].rearrange("p u j (c i) -> p u c j i", i=4),
-            )
-
-            rz_codes = keep.tile([P, UH, 2 * OUT], U32, name="rz_codes%d" % half, align_bytes=64)
-            rz_scales = keep.tile([P, UH, 2 * OUT], U8, name="rz_scales%d" % half, align_bytes=64)
-            nc.vector.quantize_mx(
-                out=rz_codes[:].rearrange("p u c -> p (u c)").bitcast(FP8X4),
-                scales=rz_scales[:].rearrange("p u c -> p (u c)"),
-                in_=rz_grouped[:].rearrange("p u g o j -> p (u g o j)"),
-            )
-            n_codes = keep.tile([P, UH, OUT], U32, name="n_codes%d" % half, align_bytes=64)
-            n_scales = keep.tile([P, UH, OUT], U8, name="n_scales%d" % half, align_bytes=64)
-            nc.vector.quantize_mx(
-                out=n_codes[:].rearrange("p u c -> p (u c)").bitcast(FP8X4),
-                scales=n_scales[:].rearrange("p u c -> p (u c)"),
-                in_=n_grouped[:].rearrange("p u o j -> p (u o j)"),
-            )
-
-            xrz_ps = sums.tile([P, UH, 2 * OUT], F32, name="xrz_ps%d" % half)
-            xn_ps = sums.tile([P, UH, OUT], F32, name="xn_ps%d" % half)
-            for codes, scales, acc in ((rz_codes, rz_scales, xrz_ps), (n_codes, n_scales, xn_ps)):
+            products = []
+            for half in range(HALVES):
+                product = bank([P, UH, OUT], F32, "x" + gate)
                 for uu in range(UH):
-                    batch = slice((half * UH + uu) * P, (half * UH + uu + 1) * P)
+                    u = half * UH + uu
                     nc.tensor.matmul_mx(
-                        out=acc[:, uu, :],
-                        lhsT=x_codes[:, batch].bitcast(FP8X4),
-                        lhsT_scale=x_scales[:, batch],
-                        rhs=codes[:, uu, :].bitcast(FP8X4),
-                        rhs_scale=scales[:, uu, :],
+                        out=product[:, uu, :],
+                        lhsT=x_codes[:, u, :].bitcast(FP8X4),
+                        lhsT_scale=x_scales[:, u, :],
+                        rhs=codes[gate][:, u, :].bitcast(FP8X4),
+                        rhs_scale=scales[gate][:, u, :],
                         start=True,
                         stop=True,
                     )
+                products.append(product)
+            return products
 
-            units = slice(half * UH, (half + 1) * UH)
-            rz = keep.tile([P, UH, 2, OUT], F32, name="rz%d" % half)
-            rz_flat = rz[:].rearrange("p u g o -> p u (g o)")
-            nc.vector.tensor_tensor(out=rz_flat, in0=xrz_ps[:], in1=hrz[half][:], op=ALU.add)
-            nc.scalar.activation(out=rz_flat, in_=rz_flat, func=ACT.Sigmoid)
-            r = rz[:, :, 0, :]
-            z = rz[:, :, 1, :]
+        def h_times_weight(gate):
+            products = []
+            for half in range(HALVES):
+                product = bank([P, UH, OUT], F32, "h" + gate)
+                for uu in range(UH):
+                    u = half * UH + uu
+                    nc.tensor.matmul(product[:, uu, :], lhsT=hT[:, u, :], rhs=wh_sb[gate][:, u, :], start=True, stop=True)
+                products.append(product)
+            return products
 
-            n = keep.tile([P, UH, OUT], F32, name="n%d" % half)
-            nc.vector.tensor_tensor(out=n[:], in0=r, in1=hn_ps[:, units, :], op=ALU.mult)
-            nc.vector.tensor_tensor(out=n[:], in0=n[:], in1=xn_ps[:], op=ALU.add)
-            nc.scalar.activation(out=n[:], in_=n[:], func=ACT.Tanh)
+        def to_sbuf(products, name):
+            copies = f32_halves(name)
+            for half in range(HALVES):
+                nc.scalar.copy(out=copies[half][:], in_=products[half][:])
+            return copies
 
-            zh = keep.tile([P, UH, OUT], F32, name="zh%d" % half)
-            h_half = h_sb[:].rearrange("b (u o) -> b u o", u=UNITS)[:, units, :]
-            nc.vector.tensor_tensor(out=zh[:], in0=z, in1=h_half, op=ALU.mult)
-            zn = keep.tile([P, UH, OUT], F32, name="zn%d" % half)
-            nc.vector.scalar_tensor_tensor(out=zn[:], in0=z, scalar=1.0, in1=n[:], op0=ALU.subtract, op1=ALU.mult)
-            result = keep.tile([P, UH, OUT], F32, name="result%d" % half)
-            nc.vector.tensor_tensor(out=result[:], in0=zh[:], in1=zn[:], op=ALU.subtract)
-            nc.sync.dma_start(out=out[:, units, :], in_=result[:])
+        x_words = x_sb[:].rearrange("b u i -> b (u i)").bitcast(F32).rearrange("b (u p v) -> b u v p", u=UNITS, v=2)
+        x_grouped = keep.tile([P, UNITS * P * PACK], BF16, align_bytes=64)
+        x_grouped_words = x_grouped[:].bitcast(F32).rearrange("p (u b v) -> p u b v", u=UNITS, v=2)
+        x_codes = keep.tile([P, UNITS, P], U32, align_bytes=64)
+        x_scales = keep.tile([P, UNITS, P], U8, align_bytes=64)
+        for half, copy in enumerate((nc.scalar.copy, nc.vector.tensor_copy)):
+            xT = bank([P, UH, 2, P], F32, "xT")
+            for uu in range(UH):
+                for v in range(2):
+                    nc.tensor.transpose(xT[:, uu, v, :], x_words[:, half * UH + uu, v, :], ident_f32[:])
+            copy(out=x_grouped_words[:, units_of(half), :, :], in_=xT[:].rearrange("p u v b -> p u b v"))
+        for half in range(HALVES):
+            nc.vector.quantize_mx(
+                out=x_codes[:, units_of(half), :].rearrange("p u b -> p (u b)").bitcast(FP8X4),
+                scales=x_scales[:, units_of(half), :].rearrange("p u b -> p (u b)"),
+                in_=x_grouped[:, half * UH * P * PACK : (half + 1) * UH * P * PACK],
+            )
+
+        regroup("r")
+
+        hT_ps = bank([P, UNITS, P], BF16, "hT_ps")
+        for u in range(UNITS):
+            nc.tensor.transpose(hT_ps[:, u, :], h_sb[:, u, :], ident_bf16[:])
+        hT = keep.tile([P, UNITS, P], BF16)
+        nc.scalar.copy(out=hT[:], in_=hT_ps[:])
+        hr = to_sbuf(h_times_weight("r"), "hr")
+        hn = h_times_weight("n")
+
+        xr = x_times_weight("r")
+        regroup("n")
+        r = f32_halves("r")
+        for half in range(HALVES):
+            nc.vector.tensor_tensor(out=r[half][:], in0=xr[half][:], in1=hr[half][:], op=ALU.add)
+            nc.scalar.activation(out=r[half][:], in_=r[half][:], func=ACT.Sigmoid)
+
+        xn = x_times_weight("n")
+        hz = to_sbuf(h_times_weight("z"), "hz")
+        regroup("z")
+        n = f32_halves("n")
+        h_minus_n = f32_halves("h_minus_n")
+        for half in range(HALVES):
+            nc.vector.tensor_tensor(out=n[half][:], in0=r[half][:], in1=hn[half][:], op=ALU.mult)
+            nc.vector.tensor_tensor(out=n[half][:], in0=n[half][:], in1=xn[half][:], op=ALU.add)
+            nc.scalar.activation(out=n[half][:], in_=n[half][:], func=ACT.Tanh)
+            nc.gpsimd.tensor_tensor(out=h_minus_n[half][:], in0=h_sb[:, units_of(half), :], in1=n[half][:], op=ALU.subtract)
+
+        xz = x_times_weight("z")
+        z = f32_halves("z")
+        for half in range(HALVES):
+            nc.vector.tensor_tensor(out=z[half][:], in0=xz[half][:], in1=hz[half][:], op=ALU.add)
+            nc.scalar.activation(out=z[half][:], in_=z[half][:], func=ACT.Sigmoid)
+        result = f32_halves("result")
+        for half in range(HALVES):
+            nc.vector.tensor_tensor(out=result[half][:], in0=z[half][:], in1=h_minus_n[half][:], op=ALU.mult)
+            nc.vector.tensor_tensor(out=result[half][:], in0=result[half][:], in1=n[half][:], op=ALU.add)
+            nc.sync.dma_start(out=out[:, units_of(half), :], in_=result[half][:])

@@ -41,29 +41,33 @@ def tile_unitwisegru_pa_s_kernel(tc, x, h, w_ir, w_iz, w_in, w_hr, w_hz, w_hn, o
         h_sb = keep.tile([P, UNITS, OUT], BF16)
         raw = {}
         wh_sb = {}
-        for gate in "rnz":
+        for gate in "rzn":
             raw[gate] = keep.tile([P, UNITS, PACK, OUT], BF16, name="raw_" + gate)
             wh_sb[gate] = keep.tile([P, UNITS, OUT], BF16, name="wh_" + gate)
 
-        def load_input_weight(gate, w):
-            for half in range(HALVES):
-                nc.sync.dma_start(
-                    out=raw[gate][:, units_of(half), :, :],
-                    in_=w[units_of(half)].rearrange("u (p j) o -> p u j o", j=PACK),
-                )
+        def load_x(half):
+            nc.sync.dma_start(out=x_sb[:, units_of(half), :], in_=x[:, units_of(half), :])
+
+        def load_input_weight(gate, w, half):
+            nc.sync.dma_start(
+                out=raw[gate][:, units_of(half), :, :],
+                in_=w[units_of(half)].rearrange("u (p j) o -> p u j o", j=PACK),
+            )
 
         def load_hidden_weight(gate, w):
             nc.sync.dma_start(out=wh_sb[gate][:], in_=w.rearrange("u k o -> k u o"))
 
         for half in range(HALVES):
-            nc.sync.dma_start(out=x_sb[:, units_of(half), :], in_=x[:, units_of(half), :])
-        load_input_weight("r", w_ir)
+            load_x(half)
+            load_input_weight("r", w_ir, half)
         nc.sync.dma_start(out=h_sb[:], in_=h)
         load_hidden_weight("r", w_hr)
         load_hidden_weight("n", w_hn)
-        load_input_weight("n", w_in)
         load_hidden_weight("z", w_hz)
-        load_input_weight("z", w_iz)
+        for half in range(HALVES):
+            load_input_weight("z", w_iz, half)
+        for half in range(HALVES):
+            load_input_weight("n", w_in, half)
 
         ident_f32 = keep.tile([P, P], F32)
         make_identity(nc, ident_f32[:])
@@ -77,43 +81,40 @@ def tile_unitwisegru_pa_s_kernel(tc, x, h, w_ir, w_iz, w_in, w_hr, w_hz, w_hn, o
         grouped = {}
         codes = {}
         scales = {}
-        for gate in "rnz":
+        for gate in "rzn":
             grouped[gate] = keep.tile([P, UNITS, OUT, PACK], BF16, name="grouped_" + gate, align_bytes=64)
             codes[gate] = keep.tile([P, UNITS, OUT], U32, name="codes_" + gate, align_bytes=64)
             scales[gate] = keep.tile([P, UNITS, OUT], U8, name="scales_" + gate, align_bytes=64)
 
-        def regroup(gate):
-            for half in range(HALVES):
-                for uu, copy in enumerate((nc.vector.tensor_copy, nc.scalar.copy)):
-                    u = half * UH + uu
-                    copy(
-                        out=grouped[gate][:, u, :, :].rearrange("p (c i) j -> p c j i", i=4),
-                        in_=raw[gate][:, u, :, :].rearrange("p j (c i) -> p c j i", i=4),
-                    )
-
-        def x_times_weight(gate):
-            for half in range(HALVES):
-                nc.vector.quantize_mx(
-                    out=codes[gate][:, units_of(half), :].rearrange("p u o -> p (u o)").bitcast(FP8X4),
-                    scales=scales[gate][:, units_of(half), :].rearrange("p u o -> p (u o)"),
-                    in_=grouped[gate][:, units_of(half), :, :].rearrange("p u o j -> p (u o j)"),
+        def regroup(gate, half):
+            for uu, copy in enumerate((nc.vector.tensor_copy, nc.scalar.copy)):
+                u = half * UH + uu
+                copy(
+                    out=grouped[gate][:, u, :, :].rearrange("p (c i) j -> p c j i", i=4),
+                    in_=raw[gate][:, u, :, :].rearrange("p j (c i) -> p c j i", i=4),
                 )
-            products = []
-            for half in range(HALVES):
-                product = bank([P, UH, OUT], F32, "x" + gate)
-                for uu in range(UH):
-                    u = half * UH + uu
-                    nc.tensor.matmul_mx(
-                        out=product[:, uu, :],
-                        lhsT=x_codes[:, u, :].bitcast(FP8X4),
-                        lhsT_scale=x_scales[:, u, :],
-                        rhs=codes[gate][:, u, :].bitcast(FP8X4),
-                        rhs_scale=scales[gate][:, u, :],
-                        start=True,
-                        stop=True,
-                    )
-                products.append(product)
-            return products
+
+        def quantise(gate, half):
+            nc.vector.quantize_mx(
+                out=codes[gate][:, units_of(half), :].rearrange("p u o -> p (u o)").bitcast(FP8X4),
+                scales=scales[gate][:, units_of(half), :].rearrange("p u o -> p (u o)"),
+                in_=grouped[gate][:, units_of(half), :, :].rearrange("p u o j -> p (u o j)"),
+            )
+
+        def x_times_weight(gate, half):
+            product = bank([P, UH, OUT], F32, "x" + gate)
+            for uu in range(UH):
+                u = half * UH + uu
+                nc.tensor.matmul_mx(
+                    out=product[:, uu, :],
+                    lhsT=x_codes[:, u, :].bitcast(FP8X4),
+                    lhsT_scale=x_scales[:, u, :],
+                    rhs=codes[gate][:, u, :].bitcast(FP8X4),
+                    rhs_scale=scales[gate][:, u, :],
+                    start=True,
+                    stop=True,
+                )
+            return product
 
         def h_times_weight(gate):
             products = []
@@ -131,6 +132,16 @@ def tile_unitwisegru_pa_s_kernel(tc, x, h, w_ir, w_iz, w_in, w_hr, w_hz, w_hn, o
                 nc.scalar.copy(out=copies[half][:], in_=products[half][:])
             return copies
 
+        def add_products(x_products, h_copies, name):
+            sums = f32_halves(name)
+            for half in range(HALVES):
+                nc.vector.tensor_tensor(out=sums[half][:], in0=x_products[half][:], in1=h_copies[half][:], op=ALU.add)
+            return sums
+
+        def sigmoid(tiles):
+            for half in range(HALVES):
+                nc.scalar.activation(out=tiles[half][:], in_=tiles[half][:], func=ACT.Sigmoid)
+
         x_words = x_sb[:].rearrange("b u i -> b (u i)").bitcast(F32).rearrange("b (u p v) -> b u v p", u=UNITS, v=2)
         x_grouped = keep.tile([P, UNITS * P * PACK], BF16, align_bytes=64)
         x_grouped_words = x_grouped[:].bitcast(F32).rearrange("p (u b v) -> p u b v", u=UNITS, v=2)
@@ -141,49 +152,62 @@ def tile_unitwisegru_pa_s_kernel(tc, x, h, w_ir, w_iz, w_in, w_hr, w_hz, w_hn, o
             for uu in range(UH):
                 for v in range(2):
                     nc.tensor.transpose(xT[:, uu, v, :], x_words[:, half * UH + uu, v, :], ident_f32[:])
+            regroup("r", half)
             copy(out=x_grouped_words[:, units_of(half), :, :], in_=xT[:].rearrange("p u v b -> p u b v"))
         for half in range(HALVES):
+            quantise("r", half)
             nc.vector.quantize_mx(
                 out=x_codes[:, units_of(half), :].rearrange("p u b -> p (u b)").bitcast(FP8X4),
                 scales=x_scales[:, units_of(half), :].rearrange("p u b -> p (u b)"),
                 in_=x_grouped[:, half * UH * P * PACK : (half + 1) * UH * P * PACK],
             )
 
-        regroup("r")
-
         hT_ps = bank([P, UNITS, P], BF16, "hT_ps")
         for u in range(UNITS):
             nc.tensor.transpose(hT_ps[:, u, :], h_sb[:, u, :], ident_bf16[:])
         hT = keep.tile([P, UNITS, P], BF16)
         nc.scalar.copy(out=hT[:], in_=hT_ps[:])
-        hr = to_sbuf(h_times_weight("r"), "hr")
+
+        hr_ps = h_times_weight("r")
+        xr = [x_times_weight("r", half) for half in range(HALVES)]
+        hz_ps = h_times_weight("z")
         hn = h_times_weight("n")
 
-        xr = x_times_weight("r")
-        regroup("n")
-        r = f32_halves("r")
         for half in range(HALVES):
-            nc.vector.tensor_tensor(out=r[half][:], in0=xr[half][:], in1=hr[half][:], op=ALU.add)
-            nc.scalar.activation(out=r[half][:], in_=r[half][:], func=ACT.Sigmoid)
+            regroup("z", half)
+        hr = to_sbuf(hr_ps, "hr")
+        for half in range(HALVES):
+            quantise("z", half)
+        xz = [x_times_weight("z", half) for half in range(HALVES)]
+        r = add_products(xr, hr, "r")
+        hz = to_sbuf(hz_ps, "hz")
 
-        xn = x_times_weight("n")
-        hz = to_sbuf(h_times_weight("z"), "hz")
-        regroup("z")
+        for half in range(HALVES):
+            regroup("n", half)
+        sigmoid(r)
+        quantise("n", 0)
+        xn = [x_times_weight("n", 0)]
+        z = add_products(xz, hz, "z")
+        sigmoid(z)
+        zh = f32_halves("zh")
+        for half in range(HALVES):
+            nc.gpsimd.tensor_tensor(out=zh[half][:], in0=z[half][:], in1=h_sb[:, units_of(half), :], op=ALU.mult)
+        quantise("n", 1)
+        xn.append(x_times_weight("n", 1))
+
+        r_hn = f32_halves("r_hn")
+        for half in range(HALVES):
+            nc.vector.tensor_tensor(out=r_hn[half][:], in0=r[half][:], in1=hn[half][:], op=ALU.mult)
         n = f32_halves("n")
-        h_minus_n = f32_halves("h_minus_n")
         for half in range(HALVES):
-            nc.vector.tensor_tensor(out=n[half][:], in0=r[half][:], in1=hn[half][:], op=ALU.mult)
-            nc.vector.tensor_tensor(out=n[half][:], in0=n[half][:], in1=xn[half][:], op=ALU.add)
+            nc.vector.tensor_tensor(out=n[half][:], in0=r_hn[half][:], in1=xn[half][:], op=ALU.add)
             nc.scalar.activation(out=n[half][:], in_=n[half][:], func=ACT.Tanh)
-            nc.gpsimd.tensor_tensor(out=h_minus_n[half][:], in0=h_sb[:, units_of(half), :], in1=n[half][:], op=ALU.subtract)
-
-        xz = x_times_weight("z")
-        z = f32_halves("z")
+        zn = f32_halves("zn")
         for half in range(HALVES):
-            nc.vector.tensor_tensor(out=z[half][:], in0=xz[half][:], in1=hz[half][:], op=ALU.add)
-            nc.scalar.activation(out=z[half][:], in_=z[half][:], func=ACT.Sigmoid)
+            nc.vector.scalar_tensor_tensor(
+                out=zn[half][:], in0=z[half][:], scalar=1.0, in1=n[half][:], op0=ALU.subtract, op1=ALU.mult
+            )
         result = f32_halves("result")
         for half in range(HALVES):
-            nc.vector.tensor_tensor(out=result[half][:], in0=z[half][:], in1=h_minus_n[half][:], op=ALU.mult)
-            nc.vector.tensor_tensor(out=result[half][:], in0=result[half][:], in1=n[half][:], op=ALU.add)
+            nc.vector.tensor_tensor(out=result[half][:], in0=zh[half][:], in1=zn[half][:], op=ALU.subtract)
             nc.sync.dma_start(out=out[:, units_of(half), :], in_=result[half][:])

@@ -28,7 +28,8 @@ def tile_unitwisegru_pa_s_kernel(tc, x, h, w_ir, w_iz, w_in, w_hr, w_hz, w_hn, o
     nc = tc.nc
     with (
         tc.tile_pool(name="keep", bufs=1) as keep,
-        tc.psum_pool(name="psum", bufs=8) as psum,
+        tc.psum_pool(name="psum", bufs=7) as psum,
+        tc.psum_pool(name="held", bufs=1) as held,
         tc.manual_schedule(),
     ):
         def bank(shape, dtype, name):
@@ -86,13 +87,15 @@ def tile_unitwisegru_pa_s_kernel(tc, x, h, w_ir, w_iz, w_in, w_hr, w_hz, w_hn, o
             codes[gate] = keep.tile([P, UNITS, OUT], U32, name="codes_" + gate, align_bytes=64)
             scales[gate] = keep.tile([P, UNITS, OUT], U8, name="scales_" + gate, align_bytes=64)
 
+        def regroup_unit(copy, gate, u):
+            copy(
+                out=grouped[gate][:, u, :, :].rearrange("p (c i) j -> p c j i", i=4),
+                in_=raw[gate][:, u, :, :].rearrange("p j (c i) -> p c j i", i=4),
+            )
+
         def regroup(gate, half):
-            for uu, copy in enumerate((nc.vector.tensor_copy, nc.scalar.copy)):
-                u = half * UH + uu
-                copy(
-                    out=grouped[gate][:, u, :, :].rearrange("p (c i) j -> p c j i", i=4),
-                    in_=raw[gate][:, u, :, :].rearrange("p j (c i) -> p c j i", i=4),
-                )
+            regroup_unit(nc.vector.tensor_copy, gate, half * UH)
+            regroup_unit(nc.scalar.copy, gate, half * UH + 1)
 
         def quantise(gate, half):
             nc.vector.quantize_mx(
@@ -101,46 +104,50 @@ def tile_unitwisegru_pa_s_kernel(tc, x, h, w_ir, w_iz, w_in, w_hr, w_hz, w_hn, o
                 in_=grouped[gate][:, units_of(half), :, :].rearrange("p u o j -> p (u o j)"),
             )
 
-        def x_times_weight(gate, half):
-            product = bank([P, UH, OUT], F32, "x" + gate)
+        def mx_passes(product, half, stationary, moving):
             for uu in range(UH):
                 u = half * UH + uu
                 nc.tensor.matmul_mx(
                     out=product[:, uu, :],
-                    lhsT=x_codes[:, u, :].bitcast(FP8X4),
-                    lhsT_scale=x_scales[:, u, :],
-                    rhs=codes[gate][:, u, :].bitcast(FP8X4),
-                    rhs_scale=scales[gate][:, u, :],
+                    lhsT=stationary[0][:, u, :].bitcast(FP8X4),
+                    lhsT_scale=stationary[1][:, u, :],
+                    rhs=moving[0][:, u, :].bitcast(FP8X4),
+                    rhs_scale=moving[1][:, u, :],
                     start=True,
                     stop=True,
                 )
             return product
 
-        def h_times_weight(gate):
-            products = []
-            for half in range(HALVES):
-                product = bank([P, UH, OUT], F32, "h" + gate)
-                for uu in range(UH):
-                    u = half * UH + uu
-                    nc.tensor.matmul(product[:, uu, :], lhsT=hT[:, u, :], rhs=wh_sb[gate][:, u, :], start=True, stop=True)
-                products.append(product)
-            return products
+        def x_times_weight(gate, half):
+            return mx_passes(bank([P, UH, OUT], F32, "x" + gate), half, (x_codes, x_scales), (codes[gate], scales[gate]))
 
-        def to_sbuf(products, name):
-            copies = f32_halves(name)
-            for half in range(HALVES):
-                nc.scalar.copy(out=copies[half][:], in_=products[half][:])
-            return copies
+        def x_times_weight_transposed(gate, half):
+            return mx_passes(bank([P, UH, P], F32, "xT" + gate), half, (codes[gate], scales[gate]), (x_codes, x_scales))
 
-        def add_products(x_products, h_copies, name):
-            sums = f32_halves(name)
-            for half in range(HALVES):
-                nc.vector.tensor_tensor(out=sums[half][:], in0=x_products[half][:], in1=h_copies[half][:], op=ALU.add)
-            return sums
+        def to_sbuf(product, name):
+            copy = keep.tile([P, UH, P], F32, name=name)
+            nc.scalar.copy(out=copy[:], in_=product[:])
+            return copy
 
-        def sigmoid(tiles):
-            for half in range(HALVES):
-                nc.scalar.activation(out=tiles[half][:], in_=tiles[half][:], func=ACT.Sigmoid)
+        def add_h_product(gate, half, x_product_transposed):
+            total = bank([P, UH, OUT], F32, "pre_" + gate)
+            for uu in range(UH):
+                u = half * UH + uu
+                nc.tensor.matmul(total[:, uu, :], lhsT=hT[:, u, :], rhs=wh_sb[gate][:, u, :], start=True, stop=False)
+                nc.tensor.matmul(
+                    total[:, uu, :],
+                    lhsT=x_product_transposed[:, uu, :],
+                    rhs=ident_f32[:],
+                    is_transpose=True,
+                    start=False,
+                    stop=True,
+                )
+            return total
+
+        def sigmoid(total, name):
+            gate_values = keep.tile([P, UH, OUT], F32, name=name)
+            nc.scalar.activation(out=gate_values[:], in_=total[:], func=ACT.Sigmoid)
+            return gate_values
 
         x_words = x_sb[:].rearrange("b u i -> b (u i)").bitcast(F32).rearrange("b (u p v) -> b u v p", u=UNITS, v=2)
         x_grouped = keep.tile([P, UNITS * P * PACK], BF16, align_bytes=64)
@@ -154,7 +161,6 @@ def tile_unitwisegru_pa_s_kernel(tc, x, h, w_ir, w_iz, w_in, w_hr, w_hz, w_hn, o
                     nc.tensor.transpose(xT[:, uu, v, :], x_words[:, half * UH + uu, v, :], ident_f32[:])
             regroup("r", half)
             copy(out=x_grouped_words[:, units_of(half), :, :], in_=xT[:].rearrange("p u v b -> p u b v"))
-        for half in range(HALVES):
             quantise("r", half)
             nc.vector.quantize_mx(
                 out=x_codes[:, units_of(half), :].rearrange("p u b -> p (u b)").bitcast(FP8X4),
@@ -168,40 +174,50 @@ def tile_unitwisegru_pa_s_kernel(tc, x, h, w_ir, w_iz, w_in, w_hr, w_hz, w_hn, o
         hT = keep.tile([P, UNITS, P], BF16)
         nc.scalar.copy(out=hT[:], in_=hT_ps[:])
 
-        hr_ps = h_times_weight("r")
-        xr = [x_times_weight("r", half) for half in range(HALVES)]
-        hz_ps = h_times_weight("z")
-        hn = h_times_weight("n")
+        xrT_ps0 = x_times_weight_transposed("r", 0)
+        hn = held.tile([P, UNITS, OUT], F32)
+        for u in range(UNITS):
+            nc.tensor.matmul(hn[:, u, :], lhsT=hT[:, u, :], rhs=wh_sb["n"][:, u, :], start=True, stop=True)
+        xrT_ps1 = x_times_weight_transposed("r", 1)
 
-        for half in range(HALVES):
-            regroup("z", half)
-        hr = to_sbuf(hr_ps, "hr")
-        for half in range(HALVES):
-            quantise("z", half)
-        xz = [x_times_weight("z", half) for half in range(HALVES)]
-        r = add_products(xr, hr, "r")
-        hz = to_sbuf(hz_ps, "hz")
+        xrT0 = to_sbuf(xrT_ps0, "xrT0")
+        regroup("z", 0)
+        regroup("z", 1)
+        xrT1 = to_sbuf(xrT_ps1, "xrT1")
+        r_sum0 = add_h_product("r", 0, xrT0)
+        quantise("z", 0)
+        regroup_unit(nc.vector.tensor_copy, "n", 0)
+        xzT_ps0 = x_times_weight_transposed("z", 0)
+        r_sum1 = add_h_product("r", 1, xrT1)
+        quantise("z", 1)
+        xzT_ps1 = x_times_weight_transposed("z", 1)
 
+        regroup_unit(nc.scalar.copy, "n", 1)
+        xzT0 = to_sbuf(xzT_ps0, "xzT0")
+        regroup_unit(nc.vector.tensor_copy, "n", 2)
+        regroup_unit(nc.vector.tensor_copy, "n", 3)
+        r = [sigmoid(r_sum0, "r0"), sigmoid(r_sum1, "r1")]
+        xzT1 = to_sbuf(xzT_ps1, "xzT1")
+        z_sum0 = add_h_product("z", 0, xzT0)
+        xn = []
         for half in range(HALVES):
-            regroup("n", half)
-        sigmoid(r)
-        quantise("n", 0)
-        xn = [x_times_weight("n", 0)]
-        z = add_products(xz, hz, "z")
-        sigmoid(z)
-        zh = f32_halves("zh")
-        for half in range(HALVES):
-            nc.gpsimd.tensor_tensor(out=zh[half][:], in0=z[half][:], in1=h_sb[:, units_of(half), :], op=ALU.mult)
-        quantise("n", 1)
-        xn.append(x_times_weight("n", 1))
+            quantise("n", half)
+            xn.append(x_times_weight("n", half))
+        z_sum1 = add_h_product("z", 1, xzT1)
+        z_sum = [z_sum0, z_sum1]
 
         r_hn = f32_halves("r_hn")
         for half in range(HALVES):
-            nc.vector.tensor_tensor(out=r_hn[half][:], in0=r[half][:], in1=hn[half][:], op=ALU.mult)
+            nc.vector.tensor_tensor(out=r_hn[half][:], in0=r[half][:], in1=hn[:, units_of(half), :], op=ALU.mult)
         n = f32_halves("n")
+        z = []
         for half in range(HALVES):
+            z.append(sigmoid(z_sum[half], "z%d" % half))
             nc.vector.tensor_tensor(out=n[half][:], in0=r_hn[half][:], in1=xn[half][:], op=ALU.add)
             nc.scalar.activation(out=n[half][:], in_=n[half][:], func=ACT.Tanh)
+        zh = f32_halves("zh")
+        for half in range(HALVES):
+            nc.gpsimd.tensor_tensor(out=zh[half][:], in0=z[half][:], in1=h_sb[:, units_of(half), :], op=ALU.mult)
         zn = f32_halves("zn")
         for half in range(HALVES):
             nc.vector.scalar_tensor_tensor(

@@ -14,8 +14,11 @@ UNITS = 4
 IN = 512
 OUT = 128
 PACK = 4
+PAIRS = PACK // 2
+RUN = 4
 HALVES = 2
 UH = UNITS // HALVES
+PSUM_BANKS = 8
 
 FLOPS = 2 * P * UNITS * (IN + OUT) * OUT * 3
 
@@ -24,11 +27,19 @@ def units_of(half):
     return slice(half * UH, (half + 1) * UH)
 
 
+def first_unit(half):
+    return half * UH
+
+
+def second_unit(half):
+    return half * UH + 1
+
+
 def tile_unitwisegru_pa_s_kernel(tc, x, h, w_ir, w_iz, w_in, w_hr, w_hz, w_hn, out):
     nc = tc.nc
     with (
         tc.tile_pool(name="keep", bufs=1) as keep,
-        tc.psum_pool(name="psum", bufs=7) as psum,
+        tc.psum_pool(name="psum", bufs=PSUM_BANKS - 1) as psum,
         tc.psum_pool(name="held", bufs=1) as held,
         tc.manual_schedule(),
     ):
@@ -87,15 +98,15 @@ def tile_unitwisegru_pa_s_kernel(tc, x, h, w_ir, w_iz, w_in, w_hr, w_hz, w_hn, o
             codes[gate] = keep.tile([P, UNITS, OUT], U32, name="codes_" + gate, align_bytes=64)
             scales[gate] = keep.tile([P, UNITS, OUT], U8, name="scales_" + gate, align_bytes=64)
 
-        def regroup_unit(copy, gate, u):
-            copy(
-                out=grouped[gate][:, u, :, :].rearrange("p (c i) j -> p c j i", i=4),
-                in_=raw[gate][:, u, :, :].rearrange("p j (c i) -> p c j i", i=4),
+        def regroup_unit(engine_copy, gate, u):
+            engine_copy(
+                out=grouped[gate][:, u, :, :].rearrange("p (c i) j -> p c j i", i=RUN),
+                in_=raw[gate][:, u, :, :].rearrange("p j (c i) -> p c j i", i=RUN),
             )
 
         def regroup(gate, half):
-            regroup_unit(nc.vector.tensor_copy, gate, half * UH)
-            regroup_unit(nc.scalar.copy, gate, half * UH + 1)
+            regroup_unit(nc.vector.tensor_copy, gate, first_unit(half))
+            regroup_unit(nc.scalar.copy, gate, second_unit(half))
 
         def quantise(gate, half):
             nc.vector.quantize_mx(
@@ -125,23 +136,31 @@ def tile_unitwisegru_pa_s_kernel(tc, x, h, w_ir, w_iz, w_in, w_hr, w_hz, w_hn, o
             return mx_passes(bank([P, UH, P], F32, "xT" + gate), half, (codes[gate], scales[gate]), (x_codes, x_scales))
 
         def to_sbuf(product, name):
-            copy = keep.tile([P, UH, P], F32, name=name)
-            nc.scalar.copy(out=copy[:], in_=product[:])
-            return copy
+            in_sbuf = keep.tile([P, UH, P], F32, name=name)
+            nc.scalar.copy(out=in_sbuf[:], in_=product[:])
+            return in_sbuf
 
         def add_h_product(gate, half, x_product_transposed):
             total = bank([P, UH, OUT], F32, "pre_" + gate)
-            for uu in range(UH):
+
+            def h_times_weight(uu, start, stop):
                 u = half * UH + uu
-                nc.tensor.matmul(total[:, uu, :], lhsT=hT[:, u, :], rhs=wh_sb[gate][:, u, :], start=True, stop=False)
+                nc.tensor.matmul(total[:, uu, :], lhsT=hT[:, u, :], rhs=wh_sb[gate][:, u, :], start=start, stop=stop)
+
+            def transpose_back(uu, start, stop):
                 nc.tensor.matmul(
                     total[:, uu, :],
                     lhsT=x_product_transposed[:, uu, :],
                     rhs=ident_f32[:],
                     is_transpose=True,
-                    start=False,
-                    stop=True,
+                    start=start,
+                    stop=stop,
                 )
+
+            h_times_weight(0, True, False)
+            transpose_back(0, False, True)
+            transpose_back(1, True, False)
+            h_times_weight(1, False, True)
             return total
 
         def sigmoid(total, name):
@@ -149,18 +168,18 @@ def tile_unitwisegru_pa_s_kernel(tc, x, h, w_ir, w_iz, w_in, w_hr, w_hz, w_hn, o
             nc.scalar.activation(out=gate_values[:], in_=total[:], func=ACT.Sigmoid)
             return gate_values
 
-        x_words = x_sb[:].rearrange("b u i -> b (u i)").bitcast(F32).rearrange("b (u p v) -> b u v p", u=UNITS, v=2)
+        x_words = x_sb[:].rearrange("b u i -> b (u i)").bitcast(F32).rearrange("b (u p v) -> b u v p", u=UNITS, v=PAIRS)
         x_grouped = keep.tile([P, UNITS * P * PACK], BF16, align_bytes=64)
-        x_grouped_words = x_grouped[:].bitcast(F32).rearrange("p (u b v) -> p u b v", u=UNITS, v=2)
+        x_grouped_words = x_grouped[:].bitcast(F32).rearrange("p (u b v) -> p u b v", u=UNITS, v=PAIRS)
         x_codes = keep.tile([P, UNITS, P], U32, align_bytes=64)
         x_scales = keep.tile([P, UNITS, P], U8, align_bytes=64)
-        for half, copy in enumerate((nc.scalar.copy, nc.vector.tensor_copy)):
-            xT = bank([P, UH, 2, P], F32, "xT")
+        for half, engine_copy in enumerate((nc.scalar.copy, nc.vector.tensor_copy)):
+            xT = bank([P, UH, PAIRS, P], F32, "xT")
             for uu in range(UH):
-                for v in range(2):
+                for v in range(PAIRS):
                     nc.tensor.transpose(xT[:, uu, v, :], x_words[:, half * UH + uu, v, :], ident_f32[:])
             regroup("r", half)
-            copy(out=x_grouped_words[:, units_of(half), :, :], in_=xT[:].rearrange("p u v b -> p u b v"))
+            engine_copy(out=x_grouped_words[:, units_of(half), :, :], in_=xT[:].rearrange("p u v b -> p u b v"))
             quantise("r", half)
             nc.vector.quantize_mx(
                 out=x_codes[:, units_of(half), :].rearrange("p u b -> p (u b)").bitcast(FP8X4),
@@ -186,16 +205,16 @@ def tile_unitwisegru_pa_s_kernel(tc, x, h, w_ir, w_iz, w_in, w_hr, w_hz, w_hn, o
         xrT1 = to_sbuf(xrT_ps1, "xrT1")
         r_sum0 = add_h_product("r", 0, xrT0)
         quantise("z", 0)
-        regroup_unit(nc.vector.tensor_copy, "n", 0)
+        regroup_unit(nc.vector.tensor_copy, "n", first_unit(0))
         xzT_ps0 = x_times_weight_transposed("z", 0)
         r_sum1 = add_h_product("r", 1, xrT1)
         quantise("z", 1)
         xzT_ps1 = x_times_weight_transposed("z", 1)
 
-        regroup_unit(nc.scalar.copy, "n", 1)
+        regroup_unit(nc.scalar.copy, "n", second_unit(0))
         xzT0 = to_sbuf(xzT_ps0, "xzT0")
-        regroup_unit(nc.vector.tensor_copy, "n", 2)
-        regroup_unit(nc.vector.tensor_copy, "n", 3)
+        regroup_unit(nc.vector.tensor_copy, "n", first_unit(1))
+        regroup_unit(nc.vector.tensor_copy, "n", second_unit(1))
         r = [sigmoid(r_sum0, "r0"), sigmoid(r_sum1, "r1")]
         xzT1 = to_sbuf(xzT_ps1, "xzT1")
         z_sum0 = add_h_product("z", 0, xzT0)

@@ -75,11 +75,11 @@ def tile_unitwisegru_pa_s_kernel(tc, x, h, w_ir, w_iz, w_in, w_hr, w_hz, w_hn, o
         nc.sync.dma_start(out=h_sb[:], in_=h)
         load_hidden_weight("r", w_hr)
         load_hidden_weight("n", w_hn)
-        load_hidden_weight("z", w_hz)
         for half in range(HALVES):
             load_input_weight("z", w_iz, half)
         for half in range(HALVES):
             load_input_weight("n", w_in, half)
+        load_hidden_weight("z", w_hz)
 
         ident_f32 = keep.tile([P, P], F32)
         make_identity(nc, ident_f32[:])

@@ -235,10 +235,9 @@ def tile_unitwisegru_pa_s_kernel(tc, x, h, w_ir, w_iz, w_in, w_hr, w_hz, w_hn, o
             nc.vector.tensor_tensor(out=n[half][:], in0=r_hn[half][:], in1=xn[half][:], op=ALU.add)
             nc.scalar.activation(out=n[half][:], in_=n[half][:], func=ACT.Tanh)
         zh = f32_halves("zh")
-        for half in range(HALVES):
-            nc.gpsimd.tensor_tensor(out=zh[half][:], in0=z[half][:], in1=h_sb[:, units_of(half), :], op=ALU.mult)
         zn = f32_halves("zn")
         for half in range(HALVES):
+            nc.vector.tensor_tensor(out=zh[half][:], in0=z[half][:], in1=h_sb[:, units_of(half), :], op=ALU.mult)
             nc.vector.scalar_tensor_tensor(
                 out=zn[half][:], in0=z[half][:], scalar=1.0, in1=n[half][:], op0=ALU.subtract, op1=ALU.mult
             )

@@ -39,8 +39,9 @@ def tile_unitwisegru_pa_s_kernel(tc, x, h, w_ir, w_iz, w_in, w_hr, w_hz, w_hn, o
     nc = tc.nc
     with (
         tc.tile_pool(name="keep", bufs=1) as keep,
-        tc.psum_pool(name="psum", bufs=PSUM_BANKS - 1) as psum,
+        tc.psum_pool(name="psum", bufs=PSUM_BANKS - 2) as psum,
         tc.psum_pool(name="held", bufs=1) as held,
+        tc.psum_pool(name="spare", bufs=1) as spare,
         tc.manual_schedule(),
     ):
         def bank(shape, dtype, name):
@@ -194,6 +195,17 @@ def tile_unitwisegru_pa_s_kernel(tc, x, h, w_ir, w_iz, w_in, w_hr, w_hz, w_hn, o
         nc.scalar.copy(out=hT[:], in_=hT_ps[:])
 
         xrT_ps0 = x_times_weight_transposed("r", 0)
+        unread = spare.tile([P, UH * OUT], F32)
+        for idle_pass in range(3):
+            nc.tensor.matmul_mx(
+                out=unread[:],
+                lhsT=x_codes[:, 0, :].bitcast(FP8X4),
+                lhsT_scale=x_scales[:, 0, :],
+                rhs=codes["r"][:, units_of(0), :].rearrange("p u o -> p (u o)").bitcast(FP8X4),
+                rhs_scale=scales["r"][:, units_of(0), :].rearrange("p u o -> p (u o)"),
+                start=True,
+                stop=True,
+            )
         hn = held.tile([P, UNITS, OUT], F32)
         for u in range(UNITS):
             nc.tensor.matmul(hn[:, u, :], lhsT=hT[:, u, :], rhs=wh_sb["n"][:, u, :], start=True, stop=True)

@@ -39,9 +39,8 @@ def tile_unitwisegru_pa_s_kernel(tc, x, h, w_ir, w_iz, w_in, w_hr, w_hz, w_hn, o
     nc = tc.nc
     with (
         tc.tile_pool(name="keep", bufs=1) as keep,
-        tc.psum_pool(name="psum", bufs=PSUM_BANKS - 2) as psum,
+        tc.psum_pool(name="psum", bufs=PSUM_BANKS - 1) as psum,
         tc.psum_pool(name="held", bufs=1) as held,
-        tc.psum_pool(name="spare", bufs=1) as spare,
         tc.manual_schedule(),
     ):
         def bank(shape, dtype, name):
@@ -70,16 +69,17 @@ def tile_unitwisegru_pa_s_kernel(tc, x, h, w_ir, w_iz, w_in, w_hr, w_hz, w_hn, o
         def load_hidden_weight(gate, w):
             nc.sync.dma_start(out=wh_sb[gate][:], in_=w.rearrange("u k o -> k u o"))
 
-        for half in range(HALVES):
-            load_x(half)
-            load_input_weight("r", w_ir, half)
+        load_x(0)
+        load_input_weight("r", w_ir, 0)
+        load_x(1)
+        load_input_weight("r", w_ir, 1)
         nc.sync.dma_start(out=h_sb[:], in_=h)
-        load_hidden_weight("r", w_hr)
-        load_hidden_weight("n", w_hn)
         for half in range(HALVES):
             load_input_weight("z", w_iz, half)
+        load_hidden_weight("r", w_hr)
         for half in range(HALVES):
             load_input_weight("n", w_in, half)
+        load_hidden_weight("n", w_hn)
         load_hidden_weight("z", w_hz)
 
         ident_f32 = keep.tile([P, P], F32)
@@ -174,66 +174,85 @@ def tile_unitwisegru_pa_s_kernel(tc, x, h, w_ir, w_iz, w_in, w_hr, w_hz, w_hn, o
         x_grouped_words = x_grouped[:].bitcast(F32).rearrange("p (u b v) -> p u b v", u=UNITS, v=PAIRS)
         x_codes = keep.tile([P, UNITS, P], U32, align_bytes=64)
         x_scales = keep.tile([P, UNITS, P], U8, align_bytes=64)
-        for half, engine_copy in enumerate((nc.scalar.copy, nc.vector.tensor_copy)):
-            xT = bank([P, UH, PAIRS, P], F32, "xT")
+        xT = {}
+
+        def transpose_x(half):
+            xT[half] = bank([P, UH, PAIRS, P], F32, "xT")
             for uu in range(UH):
                 for v in range(PAIRS):
-                    nc.tensor.transpose(xT[:, uu, v, :], x_words[:, half * UH + uu, v, :], ident_f32[:])
-            regroup("r", half)
-            engine_copy(out=x_grouped_words[:, units_of(half), :, :], in_=xT[:].rearrange("p u v b -> p u b v"))
-            quantise("r", half)
+                    nc.tensor.transpose(xT[half][:, uu, v, :], x_words[:, half * UH + uu, v, :], ident_f32[:])
+
+        def copy_x(engine_copy, half):
+            engine_copy(out=x_grouped_words[:, units_of(half), :, :], in_=xT[half][:].rearrange("p u v b -> p u b v"))
+
+        def quantise_x(half):
             nc.vector.quantize_mx(
                 out=x_codes[:, units_of(half), :].rearrange("p u b -> p (u b)").bitcast(FP8X4),
                 scales=x_scales[:, units_of(half), :].rearrange("p u b -> p (u b)"),
                 in_=x_grouped[:, half * UH * P * PACK : (half + 1) * UH * P * PACK],
             )
 
-        hT_ps = bank([P, UNITS, P], BF16, "hT_ps")
-        for u in range(UNITS):
-            nc.tensor.transpose(hT_ps[:, u, :], h_sb[:, u, :], ident_bf16[:])
+        hT_ps = {}
         hT = keep.tile([P, UNITS, P], BF16)
-        nc.scalar.copy(out=hT[:], in_=hT_ps[:])
 
-        xrT_ps0 = x_times_weight_transposed("r", 0)
-        unread = spare.tile([P, UH * OUT], F32)
-        for idle_pass in range(3):
-            nc.tensor.matmul_mx(
-                out=unread[:],
-                lhsT=x_codes[:, 0, :].bitcast(FP8X4),
-                lhsT_scale=x_scales[:, 0, :],
-                rhs=codes["r"][:, units_of(0), :].rearrange("p u o -> p (u o)").bitcast(FP8X4),
-                rhs_scale=scales["r"][:, units_of(0), :].rearrange("p u o -> p (u o)"),
-                start=True,
-                stop=True,
-            )
+        def transpose_h():
+            hT_ps[0] = bank([P, UNITS, P], BF16, "hT_ps")
+            for u in range(UNITS):
+                nc.tensor.transpose(hT_ps[0][:, u, :], h_sb[:, u, :], ident_bf16[:])
+
         hn = held.tile([P, UNITS, OUT], F32)
-        for u in range(UNITS):
-            nc.tensor.matmul(hn[:, u, :], lhsT=hT[:, u, :], rhs=wh_sb["n"][:, u, :], start=True, stop=True)
-        xrT_ps1 = x_times_weight_transposed("r", 1)
 
+        def h_times_w_hn():
+            for u in range(UNITS):
+                nc.tensor.matmul(hn[:, u, :], lhsT=hT[:, u, :], rhs=wh_sb["n"][:, u, :], start=True, stop=True)
+
+        def vec(gate, u):
+            regroup_unit(nc.vector.tensor_copy, gate, u)
+
+        def sca(gate, u):
+            regroup_unit(nc.scalar.copy, gate, u)
+
+        transpose_x(0)
+        vec("r", 1)
+        vec("r", 0)
+        copy_x(nc.scalar.copy, 0)
+        quantise("r", 0)
+        sca("r", 3)
+        vec("r", 2)
+        quantise_x(0)
+        transpose_x(1)
+        quantise("r", 1)
+        copy_x(nc.scalar.copy, 1)
+        transpose_h()
+        vec("z", 0)
+        xrT_ps0 = x_times_weight_transposed("r", 0)
+        nc.scalar.copy(out=hT[:], in_=hT_ps[0][:])
+        quantise_x(1)
         xrT0 = to_sbuf(xrT_ps0, "xrT0")
-        regroup("z", 0)
-        regroup("z", 1)
+        vec("z", 1)
+        sca("z", 2)
+        xrT_ps1 = x_times_weight_transposed("r", 1)
+        vec("z", 3)
         xrT1 = to_sbuf(xrT_ps1, "xrT1")
-        r_sum0 = add_h_product("r", 0, xrT0)
         quantise("z", 0)
-        regroup_unit(nc.vector.tensor_copy, "n", first_unit(0))
-        xzT_ps0 = x_times_weight_transposed("z", 0)
-        r_sum1 = add_h_product("r", 1, xrT1)
+        r_sum0 = add_h_product("r", 0, xrT0)
+        vec("n", 0)
         quantise("z", 1)
-        xzT_ps1 = x_times_weight_transposed("z", 1)
-
-        regroup_unit(nc.scalar.copy, "n", second_unit(0))
+        xzT_ps0 = x_times_weight_transposed("z", 0)
+        sca("n", 1)
+        r_sum1 = add_h_product("r", 1, xrT1)
         xzT0 = to_sbuf(xzT_ps0, "xzT0")
-        regroup_unit(nc.vector.tensor_copy, "n", first_unit(1))
-        regroup_unit(nc.vector.tensor_copy, "n", second_unit(1))
+        vec("n", 3)
+        vec("n", 2)
+        xzT_ps1 = x_times_weight_transposed("z", 1)
         r = [sigmoid(r_sum0, "r0"), sigmoid(r_sum1, "r1")]
         xzT1 = to_sbuf(xzT_ps1, "xzT1")
+        h_times_w_hn()
+        quantise("n", 0)
+        quantise("n", 1)
+        xn = [x_times_weight("n", 0)]
         z_sum0 = add_h_product("z", 0, xzT0)
-        xn = []
-        for half in range(HALVES):
-            quantise("n", half)
-            xn.append(x_times_weight("n", half))
+        xn.append(x_times_weight("n", 1))
         z_sum1 = add_h_product("z", 1, xzT1)
         z_sum = [z_sum0, z_sum1]
 

@@ -19,6 +19,7 @@ RUN = 4
 HALVES = 2
 UH = UNITS // HALVES
 PSUM_BANKS = 8
+IDLE_N = 256
 
 FLOPS = 2 * P * UNITS * (IN + OUT) * OUT * 3
 
@@ -39,8 +40,9 @@ def tile_unitwisegru_pa_s_kernel(tc, x, h, w_ir, w_iz, w_in, w_hr, w_hz, w_hn, o
     nc = tc.nc
     with (
         tc.tile_pool(name="keep", bufs=1) as keep,
-        tc.psum_pool(name="psum", bufs=PSUM_BANKS - 1) as psum,
+        tc.psum_pool(name="psum", bufs=PSUM_BANKS - 2) as psum,
         tc.psum_pool(name="held", bufs=1) as held,
+        tc.psum_pool(name="spare", bufs=1) as spare,
         tc.manual_schedule(),
     ):
         def bank(shape, dtype, name):
@@ -82,6 +84,26 @@ def tile_unitwisegru_pa_s_kernel(tc, x, h, w_ir, w_iz, w_in, w_hr, w_hz, w_hn, o
         load_hidden_weight("n", w_hn)
         load_hidden_weight("z", w_hz)
 
+        zero_in = keep.tile([P, IDLE_N * PACK], BF16, align_bytes=64)
+        zero_codes = keep.tile([P, IDLE_N], U32, align_bytes=64)
+        zero_scales = keep.tile([P, IDLE_N], U8, align_bytes=64)
+        nc.gpsimd.memset(zero_in[:].bitcast(F32), 0.0)
+        nc.vector.quantize_mx(out=zero_codes[:].bitcast(FP8X4), scales=zero_scales[:], in_=zero_in[:])
+        unread = spare.tile([P, IDLE_N], F32)
+
+        def idle(passes):
+            for idle_pass in range(passes):
+                nc.tensor.matmul_mx(
+                    out=unread[:],
+                    lhsT=zero_codes[:, 0:P].bitcast(FP8X4),
+                    lhsT_scale=zero_scales[:, 0:P],
+                    rhs=zero_codes[:].bitcast(FP8X4),
+                    rhs_scale=zero_scales[:],
+                    start=True,
+                    stop=True,
+                )
+
+        idle(6)
         ident_f32 = keep.tile([P, P], F32)
         make_identity(nc, ident_f32[:])
         ident_bf16 = keep.tile([P, P], BF16)
@@ -226,6 +248,7 @@ def tile_unitwisegru_pa_s_kernel(tc, x, h, w_ir, w_iz, w_in, w_hr, w_hz, w_hn, o
         transpose_h()
         vec("z", 0)
         xrT_ps0 = x_times_weight_transposed("r", 0)
+        idle(3)
         nc.scalar.copy(out=hT[:], in_=hT_ps[0][:])
         quantise_x(1)
         xrT0 = to_sbuf(xrT_ps0, "xrT0")
@@ -234,6 +257,7 @@ def tile_unitwisegru_pa_s_kernel(tc, x, h, w_ir, w_iz, w_in, w_hr, w_hz, w_hn, o
         xrT_ps1 = x_times_weight_transposed("r", 1)
         vec("z", 3)
         xrT1 = to_sbuf(xrT_ps1, "xrT1")
+        idle(1)
         quantise("z", 0)
         r_sum0 = add_h_product("r", 0, xrT0)
         vec("n", 0)

@@ -4,6 +4,7 @@ from concourse.masks import make_identity
 F32 = mybir.dt.float32
 BF16 = mybir.dt.bfloat16
 U32 = mybir.dt.uint32
+I32 = mybir.dt.int32
 U8 = mybir.dt.uint8
 FP8X4 = mybir.dt.float8_e4m3fn_x4
 ALU = mybir.AluOpType
@@ -68,8 +69,8 @@ def tile_unitwisegru_pa_s_kernel(tc, x, h, w_ir, w_iz, w_in, w_hr, w_hz, w_hn, o
                 in_=w[units_of(half)].rearrange("u (p j) o -> p u j o", j=PACK),
             )
 
-        def load_hidden_weight(gate, w):
-            nc.sync.dma_start(out=wh_sb[gate][:], in_=w.rearrange("u k o -> k u o"))
+        def load_hidden_weight(gate, w, units):
+            nc.sync.dma_start(out=wh_sb[gate][:, units, :], in_=w[units].rearrange("u k o -> k u o"))
 
         load_x(0)
         load_input_weight("r", w_ir, 0)
@@ -78,16 +79,18 @@ def tile_unitwisegru_pa_s_kernel(tc, x, h, w_ir, w_iz, w_in, w_hr, w_hz, w_hn, o
         nc.sync.dma_start(out=h_sb[:], in_=h)
         for half in range(HALVES):
             load_input_weight("z", w_iz, half)
-        load_hidden_weight("r", w_hr)
+        load_hidden_weight("r", w_hr, slice(0, UNITS))
         for half in range(HALVES):
             load_input_weight("n", w_in, half)
-        load_hidden_weight("n", w_hn)
-        load_hidden_weight("z", w_hz)
+        for half in range(HALVES):
+            load_hidden_weight("n", w_hn, units_of(half))
+        for half in range(HALVES):
+            load_hidden_weight("z", w_hz, units_of(half))
 
         zero_in = keep.tile([P, IDLE_N * PACK], BF16, align_bytes=64)
         zero_codes = keep.tile([P, IDLE_N], U32, align_bytes=64)
         zero_scales = keep.tile([P, IDLE_N], U8, align_bytes=64)
-        nc.gpsimd.memset(zero_in[:].bitcast(F32), 0.0)
+        nc.vector.memset(zero_in[:].bitcast(I32), 0)
         nc.vector.quantize_mx(out=zero_codes[:].bitcast(FP8X4), scales=zero_scales[:], in_=zero_in[:])
         unread = spare.tile([P, IDLE_N], F32)
 
@@ -103,7 +106,7 @@ def tile_unitwisegru_pa_s_kernel(tc, x, h, w_ir, w_iz, w_in, w_hr, w_hz, w_hn, o
                     stop=True,
                 )
 
-        idle(6)
+        idle(4)
         ident_f32 = keep.tile([P, P], F32)
         make_identity(nc, ident_f32[:])
         ident_bf16 = keep.tile([P, P], BF16)
@@ -199,13 +202,14 @@ def tile_unitwisegru_pa_s_kernel(tc, x, h, w_ir, w_iz, w_in, w_hr, w_hz, w_hn, o
         xT = {}
 
         def transpose_x(half):
-            xT[half] = bank([P, UH, PAIRS, P], F32, "xT")
-            for uu in range(UH):
+            for u in (first_unit(half), second_unit(half)):
+                xT[u] = bank([P, PAIRS, P], F32, "xT")
                 for v in range(PAIRS):
-                    nc.tensor.transpose(xT[half][:, uu, v, :], x_words[:, half * UH + uu, v, :], ident_f32[:])
+                    nc.tensor.transpose(xT[u][:, v, :], x_words[:, u, v, :], ident_f32[:])
 
         def copy_x(engine_copy, half):
-            engine_copy(out=x_grouped_words[:, units_of(half), :, :], in_=xT[half][:].rearrange("p u v b -> p u b v"))
+            for u in (first_unit(half), second_unit(half)):
+                engine_copy(out=x_grouped_words[:, u, :, :], in_=xT[u][:].rearrange("p v b -> p b v"))
 
         def quantise_x(half):
             nc.vector.quantize_mx(
@@ -224,8 +228,8 @@ def tile_unitwisegru_pa_s_kernel(tc, x, h, w_ir, w_iz, w_in, w_hr, w_hz, w_hn, o
 
         hn = held.tile([P, UNITS, OUT], F32)
 
-        def h_times_w_hn():
-            for u in range(UNITS):
+        def h_times_w_hn(half):
+            for u in (first_unit(half), second_unit(half)):
                 nc.tensor.matmul(hn[:, u, :], lhsT=hT[:, u, :], rhs=wh_sb["n"][:, u, :], start=True, stop=True)
 
         def vec(gate, u):
@@ -271,7 +275,8 @@ def tile_unitwisegru_pa_s_kernel(tc, x, h, w_ir, w_iz, w_in, w_hr, w_hz, w_hn, o
         xzT_ps1 = x_times_weight_transposed("z", 1)
         r = [sigmoid(r_sum0, "r0"), sigmoid(r_sum1, "r1")]
         xzT1 = to_sbuf(xzT_ps1, "xzT1")
-        h_times_w_hn()
+        h_times_w_hn(0)
+        h_times_w_hn(1)
         quantise("n", 0)
         quantise("n", 1)
         xn = [x_times_weight("n", 0)]

@@ -69,6 +69,9 @@ def tile_unitwisegru_pa_s_kernel(tc, x, h, w_ir, w_iz, w_in, w_hr, w_hz, w_hn, o
                 in_=w[units_of(half)].rearrange("u (p j) o -> p u j o", j=PACK),
             )
 
+        def load_unit(gate, w, u):
+            nc.sync.dma_start(out=raw[gate][:, u, :, :], in_=w[u].rearrange("(p j) o -> p j o", j=PACK))
+
         def load_hidden_weight(gate, w, units):
             nc.sync.dma_start(out=wh_sb[gate][:, units, :], in_=w[units].rearrange("u k o -> k u o"))
 
@@ -80,8 +83,9 @@ def tile_unitwisegru_pa_s_kernel(tc, x, h, w_ir, w_iz, w_in, w_hr, w_hz, w_hn, o
         for half in range(HALVES):
             load_input_weight("z", w_iz, half)
         load_hidden_weight("r", w_hr, slice(0, UNITS))
-        for half in range(HALVES):
-            load_input_weight("n", w_in, half)
+        load_input_weight("n", w_in, 0)
+        for u in (first_unit(1), second_unit(1)):
+            load_unit("n", w_in, u)
         for half in range(HALVES):
             load_hidden_weight("n", w_hn, units_of(half))
         for half in range(HALVES):
@@ -264,14 +268,14 @@ def tile_unitwisegru_pa_s_kernel(tc, x, h, w_ir, w_iz, w_in, w_hr, w_hz, w_hn, o
         idle(1)
         quantise("z", 0)
         r_sum0 = add_h_product("r", 0, xrT0)
-        vec("n", 0)
         quantise("z", 1)
+        vec("n", 0)
         xzT_ps0 = x_times_weight_transposed("z", 0)
         sca("n", 1)
         r_sum1 = add_h_product("r", 1, xrT1)
         xzT0 = to_sbuf(xzT_ps0, "xzT0")
-        vec("n", 3)
         vec("n", 2)
+        vec("n", 3)
         xzT_ps1 = x_times_weight_transposed("z", 1)
         r = [sigmoid(r_sum0, "r0"), sigmoid(r_sum1, "r1")]
         xzT1 = to_sbuf(xzT_ps1, "xzT1")

@@ -88,8 +88,7 @@ def tile_unitwisegru_pa_s_kernel(tc, x, h, w_ir, w_iz, w_in, w_hr, w_hz, w_hn, o
             load_unit("n", w_in, u)
         for half in range(HALVES):
             load_hidden_weight("n", w_hn, units_of(half))
-        for half in range(HALVES):
-            load_hidden_weight("z", w_hz, units_of(half))
+        load_hidden_weight("z", w_hz, slice(0, UNITS))
 
         zero_in = keep.tile([P, IDLE_N * PACK], BF16, align_bytes=64)
         zero_codes = keep.tile([P, IDLE_N], U32, align_bytes=64)

from concourse import mybir
from concourse.masks import make_identity

F32 = mybir.dt.float32
BF16 = mybir.dt.bfloat16
U32 = mybir.dt.uint32
I32 = mybir.dt.int32
U8 = mybir.dt.uint8
FP8X4 = mybir.dt.float8_e4m3fn_x4
ALU = mybir.AluOpType
ACT = mybir.ActivationFunctionType

P = 128
UNITS = 4
IN = 512
OUT = 128
PACK = 4
PAIRS = PACK // 2
RUN = 4
HALVES = 2
UH = UNITS // HALVES
PSUM_BANKS = 8
IDLE_N = 256

FLOPS = 2 * P * UNITS * (IN + OUT) * OUT * 3


def units_of(half):
    return slice(half * UH, (half + 1) * UH)


def first_unit(half):
    return half * UH


def second_unit(half):
    return half * UH + 1


def tile_unitwisegru_pa_s_kernel(tc, x, h, w_ir, w_iz, w_in, w_hr, w_hz, w_hn, out):
    nc = tc.nc
    with (
        tc.tile_pool(name="keep", bufs=1) as keep,
        tc.psum_pool(name="psum", bufs=PSUM_BANKS - 2) as psum,
        tc.psum_pool(name="held", bufs=1) as held,
        tc.psum_pool(name="spare", bufs=1) as spare,
        tc.manual_schedule(),
    ):
        def bank(shape, dtype, name):
            return psum.tile(shape, dtype, name=name, tag="bank")

        def f32_halves(name):
            return [keep.tile([P, UH, OUT], F32, name="%s%d" % (name, half)) for half in range(HALVES)]

        x_sb = keep.tile([P, UNITS, IN], BF16)
        h_sb = keep.tile([P, UNITS, OUT], BF16)
        raw = {}
        wh_sb = {}
        for gate in "rzn":
            raw[gate] = keep.tile([P, UNITS, PACK, OUT], BF16, name="raw_" + gate)
            wh_sb[gate] = keep.tile([P, UNITS, OUT], BF16, name="wh_" + gate)

        def load_x(half):
            nc.sync.dma_start(out=x_sb[:, units_of(half), :], in_=x[:, units_of(half), :])

        def load_input_weight(gate, w, half):
            nc.sync.dma_start(
                out=raw[gate][:, units_of(half), :, :],
                in_=w[units_of(half)].rearrange("u (p j) o -> p u j o", j=PACK),
            )

        def load_unit(gate, w, u):
            nc.sync.dma_start(out=raw[gate][:, u, :, :], in_=w[u].rearrange("(p j) o -> p j o", j=PACK))

        def load_hidden_weight(gate, w, units):
            nc.sync.dma_start(out=wh_sb[gate][:, units, :], in_=w[units].rearrange("u k o -> k u o"))

        load_x(0)
        load_input_weight("r", w_ir, 0)
        load_x(1)
        load_input_weight("r", w_ir, 1)
        nc.sync.dma_start(out=h_sb[:], in_=h)
        for half in range(HALVES):
            load_input_weight("z", w_iz, half)
        load_hidden_weight("r", w_hr, slice(0, UNITS))
        load_input_weight("n", w_in, 0)
        for u in (first_unit(1), second_unit(1)):
            load_unit("n", w_in, u)
        for half in range(HALVES):
            load_hidden_weight("n", w_hn, units_of(half))
        load_hidden_weight("z", w_hz, slice(0, UNITS))

        zero_in = keep.tile([P, IDLE_N * PACK], BF16, align_bytes=64)
        zero_codes = keep.tile([P, IDLE_N], U32, align_bytes=64)
        zero_scales = keep.tile([P, IDLE_N], U8, align_bytes=64)
        nc.vector.memset(zero_in[:].bitcast(I32), 0)
        nc.vector.quantize_mx(out=zero_codes[:].bitcast(FP8X4), scales=zero_scales[:], in_=zero_in[:])
        unread = spare.tile([P, IDLE_N], F32)

        def idle(passes):
            for idle_pass in range(passes):
                nc.tensor.matmul_mx(
                    out=unread[:],
                    lhsT=zero_codes[:, 0:P].bitcast(FP8X4),
                    lhsT_scale=zero_scales[:, 0:P],
                    rhs=zero_codes[:].bitcast(FP8X4),
                    rhs_scale=zero_scales[:],
                    start=True,
                    stop=True,
                )

        idle(4)
        ident_f32 = keep.tile([P, P], F32)
        make_identity(nc, ident_f32[:])
        ident_bf16 = keep.tile([P, P], BF16)
        make_identity(nc, ident_bf16[:])
        warm_in = keep.tile([P, 1], F32)
        warm_out = keep.tile([P, 1], F32)
        nc.vector.memset(warm_in[:], 0.0)
        nc.scalar.activation(out=warm_out[:], in_=warm_in[:], func=ACT.Sigmoid)

        grouped = {}
        codes = {}
        scales = {}
        for gate in "rzn":
            grouped[gate] = keep.tile([P, UNITS, OUT, PACK], BF16, name="grouped_" + gate, align_bytes=64)
            codes[gate] = keep.tile([P, UNITS, OUT], U32, name="codes_" + gate, align_bytes=64)
            scales[gate] = keep.tile([P, UNITS, OUT], U8, name="scales_" + gate, align_bytes=64)

        def regroup_unit(engine_copy, gate, u):
            engine_copy(
                out=grouped[gate][:, u, :, :].rearrange("p (c i) j -> p c j i", i=RUN),
                in_=raw[gate][:, u, :, :].rearrange("p j (c i) -> p c j i", i=RUN),
            )

        def regroup(gate, half):
            regroup_unit(nc.vector.tensor_copy, gate, first_unit(half))
            regroup_unit(nc.scalar.copy, gate, second_unit(half))

        def quantise(gate, half):
            nc.vector.quantize_mx(
                out=codes[gate][:, units_of(half), :].rearrange("p u o -> p (u o)").bitcast(FP8X4),
                scales=scales[gate][:, units_of(half), :].rearrange("p u o -> p (u o)"),
                in_=grouped[gate][:, units_of(half), :, :].rearrange("p u o j -> p (u o j)"),
            )

        def mx_passes(product, half, stationary, moving):
            for uu in range(UH):
                u = half * UH + uu
                nc.tensor.matmul_mx(
                    out=product[:, uu, :],
                    lhsT=stationary[0][:, u, :].bitcast(FP8X4),
                    lhsT_scale=stationary[1][:, u, :],
                    rhs=moving[0][:, u, :].bitcast(FP8X4),
                    rhs_scale=moving[1][:, u, :],
                    start=True,
                    stop=True,
                )
            return product

        def x_times_weight(gate, half):
            return mx_passes(bank([P, UH, OUT], F32, "x" + gate), half, (x_codes, x_scales), (codes[gate], scales[gate]))

        def x_times_weight_transposed(gate, half):
            return mx_passes(bank([P, UH, P], F32, "xT" + gate), half, (codes[gate], scales[gate]), (x_codes, x_scales))

        def to_sbuf(product, name):
            in_sbuf = keep.tile([P, UH, P], F32, name=name)
            nc.scalar.copy(out=in_sbuf[:], in_=product[:])
            return in_sbuf

        def add_h_product(gate, half, x_product_transposed):
            total = bank([P, UH, OUT], F32, "pre_" + gate)

            def h_times_weight(uu, start, stop):
                u = half * UH + uu
                nc.tensor.matmul(total[:, uu, :], lhsT=hT[:, u, :], rhs=wh_sb[gate][:, u, :], start=start, stop=stop)

            def transpose_back(uu, start, stop):
                nc.tensor.matmul(
                    total[:, uu, :],
                    lhsT=x_product_transposed[:, uu, :],
                    rhs=ident_f32[:],
                    is_transpose=True,
                    start=start,
                    stop=stop,
                )

            h_times_weight(0, True, False)
            transpose_back(0, False, True)
            transpose_back(1, True, False)
            h_times_weight(1, False, True)
            return total

        def sigmoid(total, name):
            gate_values = keep.tile([P, UH, OUT], F32, name=name)
            nc.scalar.activation(out=gate_values[:], in_=total[:], func=ACT.Sigmoid)
            return gate_values

        x_words = x_sb[:].rearrange("b u i -> b (u i)").bitcast(F32).rearrange("b (u p v) -> b u v p", u=UNITS, v=PAIRS)
        x_grouped = keep.tile([P, UNITS * P * PACK], BF16, align_bytes=64)
        x_grouped_words = x_grouped[:].bitcast(F32).rearrange("p (u b v) -> p u b v", u=UNITS, v=PAIRS)
        x_codes = keep.tile([P, UNITS, P], U32, align_bytes=64)
        x_scales = keep.tile([P, UNITS, P], U8, align_bytes=64)
        xT = {}

        def transpose_x(half):
            for u in (first_unit(half), second_unit(half)):
                xT[u] = bank([P, PAIRS, P], F32, "xT")
                for v in range(PAIRS):
                    nc.tensor.transpose(xT[u][:, v, :], x_words[:, u, v, :], ident_f32[:])

        def copy_x(engine_copy, half):
            for u in (first_unit(half), second_unit(half)):
                engine_copy(out=x_grouped_words[:, u, :, :], in_=xT[u][:].rearrange("p v b -> p b v"))

        def quantise_x(half):
            nc.vector.quantize_mx(
                out=x_codes[:, units_of(half), :].rearrange("p u b -> p (u b)").bitcast(FP8X4),
                scales=x_scales[:, units_of(half), :].rearrange("p u b -> p (u b)"),
                in_=x_grouped[:, half * UH * P * PACK : (half + 1) * UH * P * PACK],
            )

        hT_ps = {}
        hT = keep.tile([P, UNITS, P], BF16)

        def transpose_h():
            hT_ps[0] = bank([P, UNITS, P], BF16, "hT_ps")
            for u in range(UNITS):
                nc.tensor.transpose(hT_ps[0][:, u, :], h_sb[:, u, :], ident_bf16[:])

        hn = held.tile([P, UNITS, OUT], F32)

        def h_times_w_hn(half):
            for u in (first_unit(half), second_unit(half)):
                nc.tensor.matmul(hn[:, u, :], lhsT=hT[:, u, :], rhs=wh_sb["n"][:, u, :], start=True, stop=True)

        def vec(gate, u):
            regroup_unit(nc.vector.tensor_copy, gate, u)

        def sca(gate, u):
            regroup_unit(nc.scalar.copy, gate, u)

        transpose_x(0)
        vec("r", 1)
        vec("r", 0)
        copy_x(nc.scalar.copy, 0)
        quantise("r", 0)
        sca("r", 3)
        vec("r", 2)
        quantise_x(0)
        transpose_x(1)
        quantise("r", 1)
        copy_x(nc.scalar.copy, 1)
        transpose_h()
        vec("z", 0)
        xrT_ps0 = x_times_weight_transposed("r", 0)
        idle(3)
        nc.scalar.copy(out=hT[:], in_=hT_ps[0][:])
        quantise_x(1)
        xrT0 = to_sbuf(xrT_ps0, "xrT0")
        vec("z", 1)
        sca("z", 2)
        xrT_ps1 = x_times_weight_transposed("r", 1)
        vec("z", 3)
        xrT1 = to_sbuf(xrT_ps1, "xrT1")
        idle(1)
        quantise("z", 0)
        r_sum0 = add_h_product("r", 0, xrT0)
        quantise("z", 1)
        vec("n", 0)
        xzT_ps0 = x_times_weight_transposed("z", 0)
        sca("n", 1)
        r_sum1 = add_h_product("r", 1, xrT1)
        xzT0 = to_sbuf(xzT_ps0, "xzT0")
        vec("n", 2)
        vec("n", 3)
        xzT_ps1 = x_times_weight_transposed("z", 1)
        r = [sigmoid(r_sum0, "r0"), sigmoid(r_sum1, "r1")]
        xzT1 = to_sbuf(xzT_ps1, "xzT1")
        h_times_w_hn(0)
        h_times_w_hn(1)
        quantise("n", 0)
        quantise("n", 1)
        xn = [x_times_weight("n", 0)]
        z_sum0 = add_h_product("z", 0, xzT0)
        xn.append(x_times_weight("n", 1))
        z_sum1 = add_h_product("z", 1, xzT1)
        z_sum = [z_sum0, z_sum1]

        r_hn = f32_halves("r_hn")
        for half in range(HALVES):
            nc.vector.tensor_tensor(out=r_hn[half][:], in0=r[half][:], in1=hn[:, units_of(half), :], op=ALU.mult)
        n = f32_halves("n")
        z = []
        for half in range(HALVES):
            z.append(sigmoid(z_sum[half], "z%d" % half))
            nc.vector.tensor_tensor(out=n[half][:], in0=r_hn[half][:], in1=xn[half][:], op=ALU.add)
            nc.scalar.activation(out=n[half][:], in_=n[half][:], func=ACT.Tanh)
        zh = f32_halves("zh")
        zn = f32_halves("zn")
        for half in range(HALVES):
            nc.vector.tensor_tensor(out=zh[half][:], in0=z[half][:], in1=h_sb[:, units_of(half), :], op=ALU.mult)
            nc.vector.scalar_tensor_tensor(
                out=zn[half][:], in0=z[half][:], scalar=1.0, in1=n[half][:], op0=ALU.subtract, op1=ALU.mult
            )
        result = f32_halves("result")
        for half in range(HALVES):
            nc.vector.tensor_tensor(out=result[half][:], in0=zh[half][:], in1=zn[half][:], op=ALU.subtract)
            nc.sync.dma_start(out=out[:, units_of(half), :], in_=result[half][:])
